import numpy as np
import ml_dtypes


def mxq(x, axis, fmt="e4m3"):
    dtype, down = {"e4m3": (ml_dtypes.float8_e4m3fn, 7), "e5m2": (ml_dtypes.float8_e5m2, 14)}[fmt]
    v = np.moveaxis(np.asarray(x, np.float32).astype(ml_dtypes.bfloat16).astype(np.float64), axis, -1)
    blocks = v.reshape(v.shape[:-1] + (-1, 32))
    amax = np.abs(blocks).max(-1, keepdims=True)
    byte = np.maximum(np.where(amax > 0, np.frexp(amax)[1] - 1 + 127, 0) - down, 1)
    scale = np.exp2(byte - 127.0)
    codes = (blocks / scale).astype(np.float32).astype(dtype).astype(np.float64)
    return np.moveaxis((codes * scale).reshape(v.shape), -1, axis)


WIDE = False


def mx_kscale(k):
    if not WIDE:
        return np.ones(k)
    levels = np.array([10, -10, 5, -5, 0])
    a = np.random.permutation(np.resize(levels, k // 512 * 4)).reshape(k // 512, 4)
    idx = np.arange(k)
    return np.exp2(a[idx // 512, idx % 128 // 32])


BF16 = ml_dtypes.bfloat16


def bf(x):
    return np.asarray(x, np.float32).astype(BF16)


def f64(x):
    return np.asarray(x).astype(np.float64)


B, IN_F, OUT_F, N_ACT = 8192, 1024, 512, 4


def sigmoid(v):
    return 1.0 / (1.0 + np.exp(-v))


def setup_inputs():
    s = mx_kscale(IN_F)
    limit = np.sqrt(6.0 / (IN_F + OUT_F))
    return {"input": bf(np.random.standard_normal((B, IN_F)) * s),
            "W": bf(np.random.uniform(-limit, limit, (OUT_F, IN_F)) / s[None, :]),
            "b": bf(np.random.standard_normal(OUT_F) * 0.1)}


def _apply_cyclic_acts(y):
    Bb, O = y.shape
    yg = y.reshape(Bb, O // N_ACT, N_ACT)
    out = np.stack([
        np.tanh(yg[..., 0]),
        np.sin(yg[..., 1]),
        np.maximum(yg[..., 2], 0.0),
        sigmoid(yg[..., 3]),
    ], axis=-1)
    return out.reshape(Bb, O)


def reference(input, W, b):
    y = (mxq(f64(input), 1, "e4m3") @ mxq(f64(W), 1, "e4m3").T) + f64(b)
    return _apply_cyclic_acts(y)

@@ -1,0 +1,217 @@
+import math
+
+import concourse.mybir as mybir
+from concourse.masks import make_identity
+
+FLOPS = 2 * 8192 * 1024 * 512
+
+F32 = mybir.dt.float32
+BF16 = mybir.dt.bfloat16
+U32 = mybir.dt.uint32
+U8 = mybir.dt.uint8
+I32 = mybir.dt.int32
+FP8X4 = mybir.dt.float8_e4m3fn_x4
+ACT = mybir.ActivationFunctionType
+ALU = mybir.AluOpType
+
+P = 128
+K = 1024
+OUT_F = 512
+BATCH = 8192
+PASSES = K // 512
+TWO_PI = 2.0 * math.pi
+
+CHUNK_TILES = [4] * 16
+X_BUFS = 6
+LEAD = 2
+PLANE_ORDER = (0, 2, 3, 1)
+
+
+def evt_engine(r, tiles):
+    return "V" if (tiles == 4 and r == 0) else "S"
+
+
+def evo_engine(r, tiles):
+    return "V" if r < (tiles + 1) // 2 else "S"
+
+
+def tile_vdl_t_kernel(tc, x, w, b, out):
+    nc = tc.nc
+    n_chunks = len(CHUNK_TILES)
+    first_row = [P * sum(CHUNK_TILES[:s]) for s in range(n_chunks)]
+    assert P * sum(CHUNK_TILES) == BATCH
+
+    with tc.tile_pool(name="const", bufs=1) as const, \
+            tc.tile_pool(name="xin", bufs=X_BUFS) as xin, \
+            tc.tile_pool(name="grp", bufs=3) as grp, \
+            tc.tile_pool(name="cod", bufs=3) as cod, \
+            tc.tile_pool(name="act", bufs=3) as actp, \
+            tc.tile_pool(name="red", bufs=2) as red, \
+            tc.tile_pool(name="res", bufs=3) as res, \
+            tc.psum_pool(name="psum", bufs=8) as psum, \
+            tc.manual_schedule():
+
+        x_tiles = {}
+        x_codes = {}
+        x_scales = {}
+        h_tiles = {}
+        reduced_tiles = {}
+
+        def copy_out(engine, dst, src):
+            if engine == "S":
+                nc.scalar.copy(out=dst, in_=src)
+            else:
+                nc.vector.tensor_copy(out=dst, in_=src)
+
+        def quantise_rows(rows_sb, tiles, codes, scales):
+            cols = P * tiles
+            words = rows_sb.bitcast(F32)
+            grouped = grp.tile([P, PASSES * 512 * 4], BF16, align_bytes=64, tag="grouped")
+            used = grouped[:, 0:PASSES * cols * 4]
+            grouped_w = used.bitcast(F32).rearrange("q (g c u) -> q g c u", g=PASSES, u=2)
+            for r in range(tiles):
+                xt = psum.tile([P, 512], F32, tag="bank")
+                for j in range(4):
+                    nc.tensor.transpose(
+                        xt[:, P * j:P * (j + 1)],
+                        words[:, 512 * r + P * j:512 * r + P * (j + 1)],
+                        ident[:],
+                    )
+                copy_out(
+                    evt_engine(r, tiles),
+                    grouped_w[:, :, P * r:P * (r + 1), :],
+                    xt[:].rearrange("q (g u c) -> q g c u", g=PASSES, u=2),
+                )
+            nc.vector.quantize_mx(out=codes.bitcast(FP8X4), scales=scales, in_=used)
+
+        def load(s):
+            tiles = CHUNK_TILES[s]
+            x_sb = xin.tile([P, 4 * K], BF16, tag="x")
+            x_tiles[s] = x_sb
+            rows = slice(first_row[s], first_row[s] + P * tiles)
+            nc.sync.dma_start(out=x_sb[:, 0:tiles * K], in_=x[rows, :].rearrange("(p r) k -> p (r k)", r=tiles))
+
+        def stage_in(s):
+            tiles = CHUNK_TILES[s]
+            cols = P * tiles
+            codes = cod.tile([P, PASSES * 512], U32, align_bytes=64, tag="codes")
+            scales = cod.tile([P, PASSES * 512], U8, align_bytes=64, tag="scales")
+            x_codes[s] = codes
+            x_scales[s] = scales
+            quantise_rows(x_tiles[s][:, 0:tiles * K], tiles, codes[:, 0:PASSES * cols], scales[:, 0:PASSES * cols])
+
+        def stage_mx(s):
+            cols = P * CHUNK_TILES[s]
+            codes = x_codes[s]
+            scales = x_scales[s]
+            banks = {}
+            for m in PLANE_ORDER:
+                acc = psum.tile([P, 512], F32, tag="bank")
+                banks[m] = acc
+                for g in range(PASSES):
+                    wc = slice(OUT_F * g + P * m, OUT_F * g + P * (m + 1))
+                    xc = slice(cols * g, cols * (g + 1))
+                    nc.tensor.matmul_mx(
+                        out=acc[:, 0:cols],
+                        lhsT=w_codes[:, wc].bitcast(FP8X4),
+                        lhsT_scale=w_scales[:, wc],
+                        rhs=codes[:, xc].bitcast(FP8X4),
+                        rhs_scale=scales[:, xc],
+                        start=(g == 0),
+                        stop=(g == PASSES - 1),
+                    )
+            h = actp.tile([P, 4 * 512], F32, tag="h")
+            h_tiles[s] = h
+            nc.scalar.activation(
+                out=h[:, 0:cols], in_=banks[0][:, 0:cols], func=ACT.Tanh, bias=bias[:, 0:1], scale=1.0,
+            )
+            nc.vector.tensor_scalar(
+                out=h[:, 1024:1024 + cols], in0=banks[2][:, 0:cols], scalar1=bias[:, 2:3], scalar2=0.0,
+                op0=ALU.add, op1=ALU.max,
+            )
+            nc.scalar.activation(
+                out=h[:, 1536:1536 + cols], in_=banks[3][:, 0:cols], func=ACT.Tanh, bias=half_b3[:, 0:1], scale=0.5,
+            )
+            nc.gpsimd.tensor_scalar(
+                out=h[:, 1536:1536 + cols], in0=h[:, 1536:1536 + cols], scalar1=0.5, scalar2=0.5,
+                op0=ALU.mult, op1=ALU.add,
+            )
+            turns = red.tile([P, 512], I32, tag="turns")
+            nc.vector.tensor_scalar(
+                out=turns[:, 0:cols], in0=banks[1][:, 0:cols], scalar1=bias[:, 1:2], scalar2=1.0 / TWO_PI,
+                op0=ALU.add, op1=ALU.mult,
+            )
+            reduced = red.tile([P, 512], F32, tag="reduced")
+            reduced_tiles[s] = reduced
+            nc.vector.scalar_tensor_tensor(
+                out=reduced[:, 0:cols], in0=turns[:, 0:cols], scalar=-TWO_PI, in1=banks[1][:, 0:cols],
+                op0=ALU.mult, op1=ALU.add,
+            )
+
+        def stage_sin(s):
+            cols = P * CHUNK_TILES[s]
+            nc.scalar.activation(
+                out=h_tiles[s][:, 512:512 + cols], in_=reduced_tiles[s][:, 0:cols], func=ACT.Sin,
+                bias=bias[:, 1:2], scale=1.0,
+            )
+
+        def stage_out(s):
+            tiles = CHUNK_TILES[s]
+            h = h_tiles[s]
+            o_sb = res.tile([P, 4 * OUT_F], F32, tag="o")
+            for r in range(tiles):
+                ot = psum.tile([P, OUT_F], F32, tag="bank")
+                for m in range(4):
+                    nc.tensor.transpose(
+                        ot[:, P * m:P * (m + 1)],
+                        h[:, 512 * m + P * r:512 * m + P * (r + 1)],
+                        ident[:],
+                    )
+                copy_out(
+                    evo_engine(r, tiles),
+                    o_sb[:, OUT_F * r:OUT_F * (r + 1)].rearrange("p (g m) -> p g m", m=4),
+                    ot[:].rearrange("p (m g) -> p g m", m=4),
+                )
+            rows = slice(first_row[s], first_row[s] + P * tiles)
+            nc.sync.dma_start(
+                out=out[rows, :].rearrange("(p r) f -> p (r f)", r=tiles), in_=o_sb[:, 0:tiles * OUT_F],
+            )
+
+        w_sb = const.tile([P, 4 * K], BF16)
+        w_view = w.rearrange("(g m) k -> g m k", m=4)
+        for m in range(4):
+            nc.sync.dma_start(out=w_sb[:, K * m:K * (m + 1)], in_=w_view[:, m, :])
+        for s in range(min(X_BUFS, n_chunks)):
+            load(s)
+
+        bias_bf = const.tile([P, 4], BF16)
+        nc.scalar.dma_start(out=bias_bf[:], in_=b.rearrange("(g m) -> g m", m=4))
+
+        ident = const.tile([P, P], F32)
+        make_identity(nc, ident[:])
+
+        warm_in = const.tile([P, 1], F32)
+        warm_out = const.tile([P, 1], F32)
+        nc.vector.memset(warm_in[:], 0.0)
+        nc.scalar.activation(out=warm_out[:], in_=warm_in[:], func=ACT.Silu)
+
+        w_codes = const.tile([P, PASSES * OUT_F], U32, align_bytes=64)
+        w_scales = const.tile([P, PASSES * OUT_F], U8, align_bytes=64)
+        quantise_rows(w_sb[:], 4, w_codes[:], w_scales[:])
+
+        bias = const.tile([P, 4], F32)
+        nc.vector.tensor_copy(out=bias[:], in_=bias_bf[:])
+        half_b3 = const.tile([P, 1], F32)
+        nc.vector.tensor_scalar(out=half_b3[:], in0=bias[:, 3:4], scalar1=0.5, scalar2=None, op0=ALU.mult)
+
+        for i in range(-LEAD, n_chunks + 1):
+            if 0 <= i < n_chunks:
+                stage_mx(i)
+            if 0 <= i - 1 < n_chunks:
+                stage_out(i - 1)
+            if 0 <= i + LEAD < n_chunks:
+                stage_in(i + LEAD)
+                if i + LEAD + X_BUFS < n_chunks:
+                    load(i + LEAD + X_BUFS)
+            if 0 <= i < n_chunks:
+                stage_sin(i)

@@ -25,6 +25,7 @@ CHUNK_TILES = [4] * 16
 X_BUFS = 6
 LEAD = 2
 PLANE_ORDER = (0, 2, 3, 1)
+LAST_PLANE_ORDER = (1, 0, 2, 3)
 
 
 def evt_engine(r, tiles):
@@ -32,7 +33,7 @@ def evt_engine(r, tiles):
 
 
 def evo_engine(r, tiles):
-    return "V" if r < (tiles + 1) // 2 else "S"
+    return "SV"[r % 2]
 
 
 def tile_vdl_t_kernel(tc, x, w, b, out):
@@ -89,7 +90,12 @@ def tile_vdl_t_kernel(tc, x, w, b, out):
             x_sb = xin.tile([P, 4 * K], BF16, tag="x")
             x_tiles[s] = x_sb
             rows = slice(first_row[s], first_row[s] + P * tiles)
-            nc.sync.dma_start(out=x_sb[:, 0:tiles * K], in_=x[rows, :].rearrange("(p r) k -> p (r k)", r=tiles))
+            if s == 0:
+                x_view = x[rows, :].rearrange("(p r) k -> p r k", r=tiles)
+                for r in range(tiles):
+                    nc.sync.dma_start(out=x_sb[:, K * r:K * (r + 1)], in_=x_view[:, r, :])
+            else:
+                nc.sync.dma_start(out=x_sb[:, 0:tiles * K], in_=x[rows, :].rearrange("(p r) k -> p (r k)", r=tiles))
 
         def stage_in(s):
             tiles = CHUNK_TILES[s]
@@ -100,12 +106,12 @@ def tile_vdl_t_kernel(tc, x, w, b, out):
             x_scales[s] = scales
             quantise_rows(x_tiles[s][:, 0:tiles * K], tiles, codes[:, 0:PASSES * cols], scales[:, 0:PASSES * cols])
 
-        def stage_mx(s):
+        def stage_mx(s, order):
             cols = P * CHUNK_TILES[s]
             codes = x_codes[s]
             scales = x_scales[s]
             banks = {}
-            for m in PLANE_ORDER:
+            for m in order:
                 acc = psum.tile([P, 512], F32, tag="bank")
                 banks[m] = acc
                 for g in range(PASSES):
@@ -122,31 +128,30 @@ def tile_vdl_t_kernel(tc, x, w, b, out):
                     )
             h = actp.tile([P, 4 * 512], F32, tag="h")
             h_tiles[s] = h
-            nc.scalar.activation(
-                out=h[:, 0:cols], in_=banks[0][:, 0:cols], func=ACT.Tanh, bias=bias[:, 0:1], scale=1.0,
-            )
-            nc.vector.tensor_scalar(
-                out=h[:, 1024:1024 + cols], in0=banks[2][:, 0:cols], scalar1=bias[:, 2:3], scalar2=0.0,
-                op0=ALU.add, op1=ALU.max,
-            )
-            nc.scalar.activation(
-                out=h[:, 1536:1536 + cols], in_=banks[3][:, 0:cols], func=ACT.Tanh, bias=half_b3[:, 0:1], scale=0.5,
-            )
-            nc.gpsimd.tensor_scalar(
-                out=h[:, 1536:1536 + cols], in0=h[:, 1536:1536 + cols], scalar1=0.5, scalar2=0.5,
-                op0=ALU.mult, op1=ALU.add,
-            )
-            turns = red.tile([P, 512], I32, tag="turns")
-            nc.vector.tensor_scalar(
-                out=turns[:, 0:cols], in0=banks[1][:, 0:cols], scalar1=bias[:, 1:2], scalar2=1.0 / TWO_PI,
-                op0=ALU.add, op1=ALU.mult,
-            )
-            reduced = red.tile([P, 512], F32, tag="reduced")
-            reduced_tiles[s] = reduced
-            nc.vector.scalar_tensor_tensor(
-                out=reduced[:, 0:cols], in0=turns[:, 0:cols], scalar=-TWO_PI, in1=banks[1][:, 0:cols],
-                op0=ALU.mult, op1=ALU.add,
-            )
+            for m in order:
+                src_bank = banks[m][:, 0:cols]
+                dst = h[:, 512 * m:512 * m + cols]
+                if m == 0:
+                    nc.scalar.activation(out=dst, in_=src_bank, func=ACT.Tanh, bias=bias[:, 0:1], scale=1.0)
+                elif m == 2:
+                    nc.vector.tensor_scalar(
+                        out=dst, in0=src_bank, scalar1=bias[:, 2:3], scalar2=0.0, op0=ALU.add, op1=ALU.max,
+                    )
+                elif m == 3:
+                    nc.scalar.activation(out=dst, in_=src_bank, func=ACT.Tanh, bias=half_b3[:, 0:1], scale=0.5)
+                    nc.gpsimd.tensor_scalar(out=dst, in0=dst, scalar1=0.5, scalar2=0.5, op0=ALU.mult, op1=ALU.add)
+                else:
+                    turns = red.tile([P, 512], I32, tag="turns")
+                    nc.vector.tensor_scalar(
+                        out=turns[:, 0:cols], in0=src_bank, scalar1=bias[:, 1:2], scalar2=1.0 / TWO_PI,
+                        op0=ALU.add, op1=ALU.mult,
+                    )
+                    reduced = red.tile([P, 512], F32, tag="reduced")
+                    reduced_tiles[s] = reduced
+                    nc.vector.scalar_tensor_tensor(
+                        out=reduced[:, 0:cols], in0=turns[:, 0:cols], scalar=-TWO_PI, in1=src_bank,
+                        op0=ALU.mult, op1=ALU.add,
+                    )
 
         def stage_sin(s):
             cols = P * CHUNK_TILES[s]
@@ -159,6 +164,8 @@ def tile_vdl_t_kernel(tc, x, w, b, out):
             tiles = CHUNK_TILES[s]
             h = h_tiles[s]
             o_sb = res.tile([P, 4 * OUT_F], F32, tag="o")
+            rows = slice(first_row[s], first_row[s] + P * tiles)
+            out_view = out[rows, :].rearrange("(p r) f -> p r f", r=tiles)
             for r in range(tiles):
                 ot = psum.tile([P, OUT_F], F32, tag="bank")
                 for m in range(4):
@@ -172,10 +179,12 @@ def tile_vdl_t_kernel(tc, x, w, b, out):
                     o_sb[:, OUT_F * r:OUT_F * (r + 1)].rearrange("p (g m) -> p g m", m=4),
                     ot[:].rearrange("p (m g) -> p g m", m=4),
                 )
-            rows = slice(first_row[s], first_row[s] + P * tiles)
-            nc.sync.dma_start(
-                out=out[rows, :].rearrange("(p r) f -> p (r f)", r=tiles), in_=o_sb[:, 0:tiles * OUT_F],
-            )
+                if s == n_chunks - 1:
+                    nc.sync.dma_start(out=out_view[:, r, :], in_=o_sb[:, OUT_F * r:OUT_F * (r + 1)])
+            if s < n_chunks - 1:
+                nc.sync.dma_start(
+                    out=out[rows, :].rearrange("(p r) f -> p (r f)", r=tiles), in_=o_sb[:, 0:tiles * OUT_F],
+                )
 
         w_sb = const.tile([P, 4 * K], BF16)
         w_view = w.rearrange("(g m) k -> g m k", m=4)
@@ -205,13 +214,16 @@ def tile_vdl_t_kernel(tc, x, w, b, out):
         nc.vector.tensor_scalar(out=half_b3[:], in0=bias[:, 3:4], scalar1=0.5, scalar2=None, op0=ALU.mult)
 
         for i in range(-LEAD, n_chunks + 1):
+            last = (i == n_chunks - 1)
             if 0 <= i < n_chunks:
-                stage_mx(i)
+                stage_mx(i, LAST_PLANE_ORDER if last else PLANE_ORDER)
+            if last:
+                stage_sin(i)
             if 0 <= i - 1 < n_chunks:
                 stage_out(i - 1)
             if 0 <= i + LEAD < n_chunks:
                 stage_in(i + LEAD)
                 if i + LEAD + X_BUFS < n_chunks:
                     load(i + LEAD + X_BUFS)
-            if 0 <= i < n_chunks:
+            if 0 <= i < n_chunks - 1:
                 stage_sin(i)

@@ -29,7 +29,7 @@ LAST_PLANE_ORDER = (1, 0, 2, 3)
 
 
 def evt_engine(r, tiles):
-    return "V" if (tiles == 4 and r == 0) else "S"
+    return "S"
 
 
 def evo_engine(r, tiles):

@@ -24,12 +24,12 @@ TWO_PI = 2.0 * math.pi
 CHUNK_TILES = [4] * 16
 X_BUFS = 6
 LEAD = 2
-PLANE_ORDER = (0, 2, 3, 1)
-LAST_PLANE_ORDER = (1, 0, 2, 3)
+FIRST_PLANES = (1, 0)
+SECOND_PLANES = (2, 3)
 
 
 def evt_engine(r, tiles):
-    return "S"
+    return "V" if (tiles == 4 and r == 0) else "S"
 
 
 def evo_engine(r, tiles):
@@ -53,6 +53,7 @@ def tile_vdl_t_kernel(tc, x, w, b, out):
             tc.manual_schedule():
 
         x_tiles = {}
+        x_grouped = {}
         x_codes = {}
         x_scales = {}
         h_tiles = {}
@@ -64,7 +65,7 @@ def tile_vdl_t_kernel(tc, x, w, b, out):
             else:
                 nc.vector.tensor_copy(out=dst, in_=src)
 
-        def quantise_rows(rows_sb, tiles, codes, scales):
+        def transpose_rows(rows_sb, tiles):
             cols = P * tiles
             words = rows_sb.bitcast(F32)
             grouped = grp.tile([P, PASSES * 512 * 4], BF16, align_bytes=64, tag="grouped")
@@ -83,7 +84,7 @@ def tile_vdl_t_kernel(tc, x, w, b, out):
                     grouped_w[:, :, P * r:P * (r + 1), :],
                     xt[:].rearrange("q (g u c) -> q g c u", g=PASSES, u=2),
                 )
-            nc.vector.quantize_mx(out=codes.bitcast(FP8X4), scales=scales, in_=used)
+            return used
 
         def load(s):
             tiles = CHUNK_TILES[s]
@@ -99,19 +100,24 @@ def tile_vdl_t_kernel(tc, x, w, b, out):
 
         def stage_in(s):
             tiles = CHUNK_TILES[s]
-            cols = P * tiles
+            x_grouped[s] = transpose_rows(x_tiles[s][:, 0:tiles * K], tiles)
+
+        def stage_quantise(s):
+            cols = P * CHUNK_TILES[s]
             codes = cod.tile([P, PASSES * 512], U32, align_bytes=64, tag="codes")
             scales = cod.tile([P, PASSES * 512], U8, align_bytes=64, tag="scales")
             x_codes[s] = codes
             x_scales[s] = scales
-            quantise_rows(x_tiles[s][:, 0:tiles * K], tiles, codes[:, 0:PASSES * cols], scales[:, 0:PASSES * cols])
+            nc.vector.quantize_mx(
+                out=codes[:, 0:PASSES * cols].bitcast(FP8X4), scales=scales[:, 0:PASSES * cols], in_=x_grouped[s],
+            )
 
-        def stage_mx(s, order):
+        def stage_mx(s, planes):
             cols = P * CHUNK_TILES[s]
             codes = x_codes[s]
             scales = x_scales[s]
             banks = {}
-            for m in order:
+            for m in planes:
                 acc = psum.tile([P, 512], F32, tag="bank")
                 banks[m] = acc
                 for g in range(PASSES):
@@ -126,9 +132,11 @@ def tile_vdl_t_kernel(tc, x, w, b, out):
                         start=(g == 0),
                         stop=(g == PASSES - 1),
                     )
-            h = actp.tile([P, 4 * 512], F32, tag="h")
-            h_tiles[s] = h
-            for m in order:
+            if s not in h_tiles:
+                h_new = actp.tile([P, 4 * 512], F32, tag="h")
+                h_tiles[s] = h_new
+            h = h_tiles[s]
+            for m in planes:
                 src_bank = banks[m][:, 0:cols]
                 dst = h[:, 512 * m:512 * m + cols]
                 if m == 0:
@@ -206,7 +214,8 @@ def tile_vdl_t_kernel(tc, x, w, b, out):
 
         w_codes = const.tile([P, PASSES * OUT_F], U32, align_bytes=64)
         w_scales = const.tile([P, PASSES * OUT_F], U8, align_bytes=64)
-        quantise_rows(w_sb[:], 4, w_codes[:], w_scales[:])
+        w_grouped = transpose_rows(w_sb[:], 4)
+        nc.vector.quantize_mx(out=w_codes[:].bitcast(FP8X4), scales=w_scales[:], in_=w_grouped)
 
         bias = const.tile([P, 4], F32)
         nc.vector.tensor_copy(out=bias[:], in_=bias_bf[:])
@@ -214,16 +223,18 @@ def tile_vdl_t_kernel(tc, x, w, b, out):
         nc.vector.tensor_scalar(out=half_b3[:], in0=bias[:, 3:4], scalar1=0.5, scalar2=None, op0=ALU.mult)
 
         for i in range(-LEAD, n_chunks + 1):
-            last = (i == n_chunks - 1)
-            if 0 <= i < n_chunks:
-                stage_mx(i, LAST_PLANE_ORDER if last else PLANE_ORDER)
-            if last:
-                stage_sin(i)
-            if 0 <= i - 1 < n_chunks:
-                stage_out(i - 1)
-            if 0 <= i + LEAD < n_chunks:
+            now = 0 <= i < n_chunks
+            ahead = 0 <= i + LEAD < n_chunks
+            if now:
+                stage_mx(i, FIRST_PLANES)
+            if ahead:
                 stage_in(i + LEAD)
                 if i + LEAD + X_BUFS < n_chunks:
                     load(i + LEAD + X_BUFS)
-            if 0 <= i < n_chunks - 1:
+            if now:
                 stage_sin(i)
+                stage_mx(i, SECOND_PLANES)
+            if ahead:
+                stage_quantise(i + LEAD)
+            if 0 <= i - 1 < n_chunks:
+                stage_out(i - 1)

import math

import concourse.mybir as mybir
from concourse.masks import make_identity

FLOPS = 2 * 8192 * 1024 * 512

F32 = mybir.dt.float32
BF16 = mybir.dt.bfloat16
U32 = mybir.dt.uint32
U8 = mybir.dt.uint8
I32 = mybir.dt.int32
FP8X4 = mybir.dt.float8_e4m3fn_x4
ACT = mybir.ActivationFunctionType
ALU = mybir.AluOpType

P = 128
K = 1024
OUT_F = 512
BATCH = 8192
PASSES = K // 512
TWO_PI = 2.0 * math.pi

CHUNK_TILES = [4] * 16
X_BUFS = 6
LEAD = 2
FIRST_PLANES = (1, 0)
SECOND_PLANES = (2, 3)


def evt_engine(r, tiles):
    return "V" if (tiles == 4 and r == 0) else "S"


def evo_engine(r, tiles):
    return "SV"[r % 2]


def tile_vdl_t_kernel(tc, x, w, b, out):
    nc = tc.nc
    n_chunks = len(CHUNK_TILES)
    first_row = [P * sum(CHUNK_TILES[:s]) for s in range(n_chunks)]
    assert P * sum(CHUNK_TILES) == BATCH

    with tc.tile_pool(name="const", bufs=1) as const, \
            tc.tile_pool(name="xin", bufs=X_BUFS) as xin, \
            tc.tile_pool(name="grp", bufs=3) as grp, \
            tc.tile_pool(name="cod", bufs=3) as cod, \
            tc.tile_pool(name="act", bufs=3) as actp, \
            tc.tile_pool(name="red", bufs=2) as red, \
            tc.tile_pool(name="res", bufs=3) as res, \
            tc.psum_pool(name="psum", bufs=8) as psum, \
            tc.manual_schedule():

        x_tiles = {}
        x_grouped = {}
        x_codes = {}
        x_scales = {}
        h_tiles = {}
        reduced_tiles = {}

        def copy_out(engine, dst, src):
            if engine == "S":
                nc.scalar.copy(out=dst, in_=src)
            else:
                nc.vector.tensor_copy(out=dst, in_=src)

        def transpose_rows(rows_sb, tiles):
            cols = P * tiles
            words = rows_sb.bitcast(F32)
            grouped = grp.tile([P, PASSES * 512 * 4], BF16, align_bytes=64, tag="grouped")
            used = grouped[:, 0:PASSES * cols * 4]
            grouped_w = used.bitcast(F32).rearrange("q (g c u) -> q g c u", g=PASSES, u=2)
            for r in range(tiles):
                xt = psum.tile([P, 512], F32, tag="bank")
                for j in range(4):
                    nc.tensor.transpose(
                        xt[:, P * j:P * (j + 1)],
                        words[:, 512 * r + P * j:512 * r + P * (j + 1)],
                        ident[:],
                    )
                copy_out(
                    evt_engine(r, tiles),
                    grouped_w[:, :, P * r:P * (r + 1), :],
                    xt[:].rearrange("q (g u c) -> q g c u", g=PASSES, u=2),
                )
            return used

        def load(s):
            tiles = CHUNK_TILES[s]
            x_sb = xin.tile([P, 4 * K], BF16, tag="x")
            x_tiles[s] = x_sb
            rows = slice(first_row[s], first_row[s] + P * tiles)
            if s == 0:
                x_view = x[rows, :].rearrange("(p r) k -> p r k", r=tiles)
                for r in range(tiles):
                    nc.sync.dma_start(out=x_sb[:, K * r:K * (r + 1)], in_=x_view[:, r, :])
            else:
                nc.sync.dma_start(out=x_sb[:, 0:tiles * K], in_=x[rows, :].rearrange("(p r) k -> p (r k)", r=tiles))

        def stage_in(s):
            tiles = CHUNK_TILES[s]
            x_grouped[s] = transpose_rows(x_tiles[s][:, 0:tiles * K], tiles)

        def stage_quantise(s):
            cols = P * CHUNK_TILES[s]
            codes = cod.tile([P, PASSES * 512], U32, align_bytes=64, tag="codes")
            scales = cod.tile([P, PASSES * 512], U8, align_bytes=64, tag="scales")
            x_codes[s] = codes
            x_scales[s] = scales
            nc.vector.quantize_mx(
                out=codes[:, 0:PASSES * cols].bitcast(FP8X4), scales=scales[:, 0:PASSES * cols], in_=x_grouped[s],
            )

        def stage_mx(s, planes):
            cols = P * CHUNK_TILES[s]
            codes = x_codes[s]
            scales = x_scales[s]
            banks = {}
            for m in planes:
                acc = psum.tile([P, 512], F32, tag="bank")
                banks[m] = acc
                for g in range(PASSES):
                    wc = slice(OUT_F * g + P * m, OUT_F * g + P * (m + 1))
                    xc = slice(cols * g, cols * (g + 1))
                    nc.tensor.matmul_mx(
                        out=acc[:, 0:cols],
                        lhsT=w_codes[:, wc].bitcast(FP8X4),
                        lhsT_scale=w_scales[:, wc],
                        rhs=codes[:, xc].bitcast(FP8X4),
                        rhs_scale=scales[:, xc],
                        start=(g == 0),
                        stop=(g == PASSES - 1),
                    )
            if s not in h_tiles:
                h_new = actp.tile([P, 4 * 512], F32, tag="h")
                h_tiles[s] = h_new
            h = h_tiles[s]
            for m in planes:
                src_bank = banks[m][:, 0:cols]
                dst = h[:, 512 * m:512 * m + cols]
                if m == 0:
                    nc.scalar.activation(out=dst, in_=src_bank, func=ACT.Tanh, bias=bias[:, 0:1], scale=1.0)
                elif m == 2:
                    nc.vector.tensor_scalar(
                        out=dst, in0=src_bank, scalar1=bias[:, 2:3], scalar2=0.0, op0=ALU.add, op1=ALU.max,
                    )
                elif m == 3:
                    nc.scalar.activation(out=dst, in_=src_bank, func=ACT.Tanh, bias=half_b3[:, 0:1], scale=0.5)
                    nc.gpsimd.tensor_scalar(out=dst, in0=dst, scalar1=0.5, scalar2=0.5, op0=ALU.mult, op1=ALU.add)
                else:
                    turns = red.tile([P, 512], I32, tag="turns")
                    nc.vector.tensor_scalar(
                        out=turns[:, 0:cols], in0=src_bank, scalar1=bias[:, 1:2], scalar2=1.0 / TWO_PI,
                        op0=ALU.add, op1=ALU.mult,
                    )
                    reduced = red.tile([P, 512], F32, tag="reduced")
                    reduced_tiles[s] = reduced
                    nc.vector.scalar_tensor_tensor(
                        out=reduced[:, 0:cols], in0=turns[:, 0:cols], scalar=-TWO_PI, in1=src_bank,
                        op0=ALU.mult, op1=ALU.add,
                    )

        def stage_sin(s):
            cols = P * CHUNK_TILES[s]
            nc.scalar.activation(
                out=h_tiles[s][:, 512:512 + cols], in_=reduced_tiles[s][:, 0:cols], func=ACT.Sin,
                bias=bias[:, 1:2], scale=1.0,
            )

        def stage_out(s):
            tiles = CHUNK_TILES[s]
            h = h_tiles[s]
            o_sb = res.tile([P, 4 * OUT_F], F32, tag="o")
            rows = slice(first_row[s], first_row[s] + P * tiles)
            out_view = out[rows, :].rearrange("(p r) f -> p r f", r=tiles)
            for r in range(tiles):
                ot = psum.tile([P, OUT_F], F32, tag="bank")
                for m in range(4):
                    nc.tensor.transpose(
                        ot[:, P * m:P * (m + 1)],
                        h[:, 512 * m + P * r:512 * m + P * (r + 1)],
                        ident[:],
                    )
                copy_out(
                    evo_engine(r, tiles),
                    o_sb[:, OUT_F * r:OUT_F * (r + 1)].rearrange("p (g m) -> p g m", m=4),
                    ot[:].rearrange("p (m g) -> p g m", m=4),
                )
                if s == n_chunks - 1:
                    nc.sync.dma_start(out=out_view[:, r, :], in_=o_sb[:, OUT_F * r:OUT_F * (r + 1)])
            if s < n_chunks - 1:
                nc.sync.dma_start(
                    out=out[rows, :].rearrange("(p r) f -> p (r f)", r=tiles), in_=o_sb[:, 0:tiles * OUT_F],
                )

        w_sb = const.tile([P, 4 * K], BF16)
        w_view = w.rearrange("(g m) k -> g m k", m=4)
        for m in range(4):
            nc.sync.dma_start(out=w_sb[:, K * m:K * (m + 1)], in_=w_view[:, m, :])
        for s in range(min(X_BUFS, n_chunks)):
            load(s)

        bias_bf = const.tile([P, 4], BF16)
        nc.scalar.dma_start(out=bias_bf[:], in_=b.rearrange("(g m) -> g m", m=4))

        ident = const.tile([P, P], F32)
        make_identity(nc, ident[:])

        warm_in = const.tile([P, 1], F32)
        warm_out = const.tile([P, 1], F32)
        nc.vector.memset(warm_in[:], 0.0)
        nc.scalar.activation(out=warm_out[:], in_=warm_in[:], func=ACT.Silu)

        w_codes = const.tile([P, PASSES * OUT_F], U32, align_bytes=64)
        w_scales = const.tile([P, PASSES * OUT_F], U8, align_bytes=64)
        w_grouped = transpose_rows(w_sb[:], 4)
        nc.vector.quantize_mx(out=w_codes[:].bitcast(FP8X4), scales=w_scales[:], in_=w_grouped)

        bias = const.tile([P, 4], F32)
        nc.vector.tensor_copy(out=bias[:], in_=bias_bf[:])
        half_b3 = const.tile([P, 1], F32)
        nc.vector.tensor_scalar(out=half_b3[:], in0=bias[:, 3:4], scalar1=0.5, scalar2=None, op0=ALU.mult)

        for i in range(-LEAD, n_chunks + 1):
            now = 0 <= i < n_chunks
            ahead = 0 <= i + LEAD < n_chunks
            if now:
                stage_mx(i, FIRST_PLANES)
            if ahead:
                stage_in(i + LEAD)
                if i + LEAD + X_BUFS < n_chunks:
                    load(i + LEAD + X_BUFS)
            if now:
                stage_sin(i)
                stage_mx(i, SECOND_PLANES)
            if ahead:
                stage_quantise(i + LEAD)
            if 0 <= i - 1 < n_chunks:
                stage_out(i - 1)
